import numpy as np
import ml_dtypes


BF16 = ml_dtypes.bfloat16


def bf(x):
    return np.asarray(x, np.float32).astype(BF16)


def f64(x):
    return np.asarray(x).astype(np.float64)


E2M1 = np.array([0.0, 0.5, 1.0, 1.5, 2.0, 3.0, 4.0, 6.0, -0.0, -0.5, -1.0, -1.5, -2.0, -3.0, -4.0, -6.0])


def pack_weight(w, fmt):
    k, n = w.shape
    w = f64(bf(w)).reshape(k // 32, 32, n)
    amax = np.abs(w).max(1)
    if fmt == "e4m3":
        byte = np.frexp(amax)[1] - 1 + 127 - 7
    else:
        mant, ex = np.frexp(amax / 6.0)
        byte = np.where(mant > 0.5, ex, ex - 1) + 127
    byte = np.clip(np.where(amax > 0, byte, 1), 1, 254)
    scaled = (w * np.exp2(127.0 - byte)[:, None, :]).reshape(k, n).astype(np.float32)
    by_word = np.ascontiguousarray(scaled.reshape(k // 512, 128, 4, n).transpose(0, 1, 3, 2))
    if fmt == "e4m3":
        words = by_word.astype(ml_dtypes.float8_e4m3fn).view(np.uint8)
    else:
        c = by_word.astype(ml_dtypes.float4_e2m1fn).view(np.uint8) & 0xF
        words = c[..., 0::2] | (c[..., 1::2] << 4)
    return np.ascontiguousarray(words), np.ascontiguousarray(byte.astype(np.uint8).reshape(k // 512, 16, n))


def unpack_weight(words, scales, fmt):
    g, p, n, _ = words.shape
    if fmt == "e4m3":
        vals = np.ascontiguousarray(words).view(ml_dtypes.float8_e4m3fn).astype(np.float64)
    else:
        nib = np.empty((g, p, n, 4), np.uint8)
        nib[..., 0::2] = words & 0xF
        nib[..., 1::2] = words >> 4
        vals = E2M1[nib]
    vals = vals * np.repeat(np.exp2(scales.astype(np.float64) - 127.0), 8, axis=1)[..., None]
    return vals.transpose(0, 1, 3, 2).reshape(g * 512, n)

def pack4(w):
    words, scales = pack_weight(w, "e2m1")
    return words.reshape(words.shape[0], 128, -1), scales


def unpack4(words, scales):
    return unpack_weight(words.reshape(words.shape[0], 128, -1, 2), scales, "e2m1")


def kspread(k):
    return np.exp2(np.repeat(np.random.randint(-6, 7, k // 32), 32).astype(np.float64))


B, T, C, H = 4, 128, 4096, 32
HD = C // H


def rotary_pos_emb(v):
    exponents = f64(np.arange(0, HD, 2)[: HD // 2] // HD)
    freqs = 1.0 / np.power(1000.0, exponents)
    theta = f64(np.arange(T))[:, None] * freqs[None, :]
    cos = np.cos(theta)[None, :, None, :]
    sin = np.sin(theta)[None, :, None, :]
    vr = v.reshape(B, T, H, HD // 2, 2)
    v0, v1 = vr[..., 0], vr[..., 1]
    out = np.stack([v0 * cos - v1 * sin, v0 * sin + v1 * cos], axis=-1)
    return out.reshape(B, T, H, HD)


def setup_inputs():
    s = kspread(C)
    x = np.random.standard_normal((B, T, C)) * s
    wq = np.random.standard_normal((C, C)) / np.sqrt(C) / s[None, :]
    wk = np.random.standard_normal((C, C)) / np.sqrt(C) / s[None, :]
    x_words, x_scales = pack4(np.ascontiguousarray(x.reshape(B * T, C).T))
    wq_words, wq_scales = pack4(np.ascontiguousarray(wq.T))
    wk_words, wk_scales = pack4(np.ascontiguousarray(wk.T))
    return {"x_words": x_words, "x_scales": x_scales,
            "wq_words": wq_words, "wq_scales": wq_scales,
            "wk_words": wk_words, "wk_scales": wk_scales}


def reference(x_words, x_scales, wq_words, wq_scales, wk_words, wk_scales):
    xm = unpack4(x_words, x_scales).T.reshape(B, T, C)
    q = (xm @ unpack4(wq_words, wq_scales)).reshape(B, T, H, HD)
    k = (xm @ unpack4(wk_words, wk_scales)).reshape(B, T, H, HD)
    return rotary_pos_emb(q), rotary_pos_emb(k)

@@ -1,0 +1,212 @@
+import math
+from contextlib import ExitStack
+
+import concourse.mybir as mybir
+
+F32 = mybir.dt.float32
+I32 = mybir.dt.int32
+U8 = mybir.dt.uint8
+FP4X4 = mybir.dt.float4_e2m1fn_x4
+ALU = mybir.AluOpType
+ACT = mybir.ActivationFunctionType
+
+P = 128
+PASSES = 8
+TOKEN_TILES = 4
+CHANNELS = 4096
+N_TILE = 512
+BLOCKS = CHANNELS // N_TILE
+ANGLE_BITS = 8
+
+FLOPS = 2 * 512 * 4096 * 2 * CHANNELS
+
+
+def tile_attention_pa_kernel(
+    tc, x_words, x_scales, wq_words, wq_scales, wk_words, wk_scales, out_0, out_1
+):
+    nc = tc.nc
+    w_words = (wq_words, wk_words)
+    w_scales = (wq_scales, wk_scales)
+    outs = (out_0, out_1)
+
+    with ExitStack() as ctx:
+        keep = ctx.enter_context(tc.tile_pool(name="keep", bufs=1))
+        small = ctx.enter_context(tc.tile_pool(name="small", bufs=1))
+        turned = ctx.enter_context(tc.tile_pool(name="turned", bufs=1))
+        result = ctx.enter_context(tc.tile_pool(name="result", bufs=1))
+        psum = ctx.enter_context(tc.psum_pool(name="psum", bufs=1))
+        ctx.enter_context(tc.manual_schedule())
+
+        def load_codes(tile_ap, dram_ap):
+            nc.sync.dma_start(out=tile_ap.bitcast(I32), in_=dram_ap.bitcast(I32))
+
+        def load_scales(name, dram, g0, g1, c0, c1):
+            plane = keep.tile([P, g1 - g0, c1 - c0], U8, name=name, align_bytes=64)
+            nc.vector.memset(plane[:].bitcast(I32), 0)
+            for q in (0, 2, 1, 3):
+                nc.sync.dma_start(
+                    out=plane[32 * q : 32 * q + 4, :, :].bitcast(I32),
+                    in_=dram[g0:g1, 4 * q : 4 * q + 4, c0:c1].rearrange("g r n -> r g n").bitcast(I32),
+                )
+            return plane
+
+        x_codes = {}
+        x_planes = {}
+        w_codes = {}
+        w_planes = {}
+
+        position = small.tile([P, ANGLE_BITS], I32, name="position")
+        nc.gpsimd.iota(position[:], pattern=[[0, ANGLE_BITS]], base=0, channel_multiplier=1)
+        digit_no = small.tile([P, ANGLE_BITS], I32, name="digit_no")
+        nc.gpsimd.iota(digit_no[:], pattern=[[1, ANGLE_BITS]], base=0, channel_multiplier=0)
+
+        HEAD_BLOCKS = 2
+        HEAD_COLS = HEAD_BLOCKS * N_TILE
+
+        def load_head_codes(g):
+            xc = keep.tile([P, 2 * 512], U8, name="x_codes%d" % g, align_bytes=64)
+            load_codes(xc[:], x_words[g])
+            x_codes[g] = xc
+            wc = keep.tile([P, 2 * HEAD_COLS], U8, name="head_codes%d" % g, align_bytes=64)
+            load_codes(wc[:], wq_words[g][:, 0 : 2 * HEAD_COLS])
+            for n in range(HEAD_BLOCKS):
+                w_codes[(0, n, g)] = wc[:, 2 * N_TILE * n : 2 * N_TILE * (n + 1)]
+
+        def load_head_scales(g0, g1):
+            xp = load_scales("x_planes%d" % g0, x_scales, g0, g1, 0, 512)
+            wp = load_scales("head_planes%d" % g0, wq_scales, g0, g1, 0, HEAD_COLS)
+            for g in range(g0, g1):
+                x_planes[g] = xp[:, g - g0, :]
+                for n in range(HEAD_BLOCKS):
+                    w_planes[(0, n, g)] = wp[:, g - g0, N_TILE * n : N_TILE * (n + 1)]
+
+        load_head_codes(0)
+        load_head_scales(0, 2)
+        load_head_codes(1)
+        load_head_scales(2, PASSES)
+        for g in range(2, PASSES):
+            load_head_codes(g)
+
+        def load_chunk(w, n0, blocks):
+            c0 = N_TILE * n0
+            c1 = N_TILE * (n0 + blocks)
+            wp = load_scales("planes%d_%d" % (w, n0), w_scales[w], 0, PASSES, c0, c1)
+            wc = keep.tile([P, PASSES, 2 * (c1 - c0)], U8, name="codes%d_%d" % (w, n0), align_bytes=64)
+            load_codes(wc[:], w_words[w][:, :, 2 * c0 : 2 * c1].rearrange("g p c -> p g c"))
+            for n in range(blocks):
+                for g in range(PASSES):
+                    w_codes[(w, n0 + n, g)] = wc[:, g, 2 * N_TILE * n : 2 * N_TILE * (n + 1)]
+                    w_planes[(w, n0 + n, g)] = wp[:, g, N_TILE * n : N_TILE * (n + 1)]
+
+        load_chunk(0, 2, 2)
+
+        shifted = small.tile([P, ANGLE_BITS], I32, name="shifted")
+        nc.vector.tensor_tensor(out=shifted[:], in0=position[:], in1=digit_no[:], op=ALU.logical_shift_right)
+        digit_i = small.tile([P, ANGLE_BITS], I32, name="digit_i")
+        nc.vector.tensor_scalar(out=digit_i[:], in0=shifted[:], scalar1=1, scalar2=None, op0=ALU.bitwise_and)
+        digit = small.tile([P, ANGLE_BITS], F32, name="digit")
+        nc.vector.tensor_copy(out=digit[:], in_=digit_i[:])
+        re = small.tile([P, ANGLE_BITS], F32, name="re8")
+        im = small.tile([P, ANGLE_BITS], F32, name="im8")
+        for b in range(ANGLE_BITS):
+            angle = 2.0**b
+            nc.vector.tensor_scalar(
+                out=re[:, b : b + 1], in0=digit[:, b : b + 1],
+                scalar1=math.cos(angle) - 1.0, scalar2=1.0, op0=ALU.mult, op1=ALU.add,
+            )
+            nc.vector.tensor_scalar(
+                out=im[:, b : b + 1], in0=digit[:, b : b + 1],
+                scalar1=math.sin(angle), scalar2=None, op0=ALU.mult,
+            )
+        width = ANGLE_BITS // 2
+        while width >= 1:
+            a_re, a_im = re[:, 0:width], im[:, 0:width]
+            b_re, b_im = re[:, width : 2 * width], im[:, width : 2 * width]
+            rr = small.tile([P, width], F32, name="rr%d" % width)
+            ii = small.tile([P, width], F32, name="ii%d" % width)
+            ri = small.tile([P, width], F32, name="ri%d" % width)
+            ir = small.tile([P, width], F32, name="ir%d" % width)
+            nc.vector.tensor_tensor(out=rr[:], in0=a_re, in1=b_re, op=ALU.mult)
+            nc.vector.tensor_tensor(out=ii[:], in0=a_im, in1=b_im, op=ALU.mult)
+            nc.vector.tensor_tensor(out=ri[:], in0=a_re, in1=b_im, op=ALU.mult)
+            nc.vector.tensor_tensor(out=ir[:], in0=a_im, in1=b_re, op=ALU.mult)
+            re = small.tile([P, width], F32, name="re%d" % width)
+            im = small.tile([P, width], F32, name="im%d" % width)
+            nc.vector.tensor_tensor(out=re[:], in0=rr[:], in1=ii[:], op=ALU.subtract)
+            nc.vector.tensor_tensor(out=im[:], in0=ri[:], in1=ir[:], op=ALU.add)
+            width //= 2
+        cos_p = re
+        sin_p = im
+        neg_sin_p = small.tile([P, 1], F32, name="neg_sin_p")
+        nc.scalar.activation(out=neg_sin_p[:], in_=sin_p[:], func=ACT.Copy, scale=-1.0)
+
+        counts = {"bank": 0, "cross": 0, "rot": 0}
+
+        def turn(kind, slots):
+            counts[kind] += 1
+            return "%s%d" % (kind, (counts[kind] - 1) % slots)
+
+        def new_bank(cols):
+            tag = turn("bank", 8)
+            acc = psum.tile([P, cols], F32, name=tag, tag=tag)
+            return acc
+
+        def multiply(acc, w, n, m, g, c0, cols):
+            nc.tensor.matmul_mx(
+                out=acc[:],
+                lhsT=x_codes[g][:, 2 * P * m : 2 * P * (m + 1)].bitcast(FP4X4),
+                lhsT_scale=x_planes[g][:, P * m : P * (m + 1)],
+                rhs=w_codes[(w, n, g)][:, 2 * c0 : 2 * (c0 + cols)].bitcast(FP4X4),
+                rhs_scale=w_planes[(w, n, g)][:, c0 : c0 + cols],
+                start=(g == 0),
+                stop=(g == PASSES - 1),
+            )
+
+        def rotate_and_store(acc, w, n, m, c0, cols):
+            half = cols // 2
+            tag = turn("cross", 3)
+            cross = turned.tile([P, 2, half], F32, name=tag, tag=tag)
+            nc.scalar.activation(out=cross[:, 0, :], in_=acc[:, 1:cols:2], func=ACT.Copy, scale=neg_sin_p[:, 0:1])
+            nc.scalar.activation(out=cross[:, 1, :], in_=acc[:, 0:cols:2], func=ACT.Copy, scale=sin_p[:, 0:1])
+            tag = turn("rot", 8)
+            rot = result.tile([P, cols], F32, name=tag, tag=tag)
+            nc.vector.scalar_tensor_tensor(
+                out=rot[:].rearrange("p (i j) -> p i j", j=2),
+                in0=acc[:].rearrange("p (i j) -> p i j", j=2),
+                scalar=cos_p[:, 0:1],
+                in1=cross[:].rearrange("p j i -> p i j"),
+                op0=ALU.mult,
+                op1=ALU.add,
+            )
+            queue = nc.sync if (w, n) == (1, BLOCKS - 1) else nc.gpsimd
+            first = N_TILE * n + c0
+            queue.dma_start(
+                out=outs[w][m].rearrange("t h d -> t (h d)")[:, first : first + cols],
+                in_=rot[:],
+            )
+
+        head = [(n, m) for n in range(HEAD_BLOCKS) for m in range(TOKEN_TILES)]
+        banks = {}
+        for nm in head:
+            banks[nm] = new_bank(N_TILE)
+        for g in range(PASSES):
+            for n, m in head:
+                multiply(banks[(n, m)], 0, n, m, g, 0, N_TILE)
+        for n, m in head:
+            rotate_and_store(banks[(n, m)], 0, n, m, 0, N_TILE)
+            if (n, m) == (0, 0):
+                load_chunk(0, 4, 2)
+
+        rest = [(0, n) for n in range(HEAD_BLOCKS, BLOCKS)] + [(1, n) for n in range(BLOCKS)]
+        for w, n in rest:
+            for m in range(TOKEN_TILES):
+                last = (w, n, m) == (1, BLOCKS - 1, TOKEN_TILES - 1)
+                cols = N_TILE // 2 if last else N_TILE
+                for c0 in range(0, N_TILE, cols):
+                    acc = new_bank(cols)
+                    for g in range(PASSES):
+                        multiply(acc, w, n, m, g, c0, cols)
+                    rotate_and_store(acc, w, n, m, c0, cols)
+                sweep = BLOCKS * w + n
+                if m == 0 and sweep % 2 == 1 and sweep + 3 < 2 * BLOCKS:
+                    load_chunk((sweep + 3) // BLOCKS, (sweep + 3) % BLOCKS, 2)

@@ -4,6 +4,7 @@ from contextlib import ExitStack
 import concourse.mybir as mybir
 
 F32 = mybir.dt.float32
+BF16 = mybir.dt.bfloat16
 I32 = mybir.dt.int32
 U8 = mybir.dt.uint8
 FP4X4 = mybir.dt.float4_e2m1fn_x4
@@ -17,6 +18,7 @@ CHANNELS = 4096
 N_TILE = 512
 BLOCKS = CHANNELS // N_TILE
 ANGLE_BITS = 8
+WARM_UP = 10
 
 FLOPS = 2 * 512 * 4096 * 2 * CHANNELS
 
@@ -55,6 +57,9 @@ def tile_attention_pa_kernel(
         w_codes = {}
         w_planes = {}
 
+        zeros = small.tile([P, N_TILE], BF16, name="zeros")
+        nc.gpsimd.memset(zeros[:], 0.0)
+
         position = small.tile([P, ANGLE_BITS], I32, name="position")
         nc.gpsimd.iota(position[:], pattern=[[0, ANGLE_BITS]], base=0, channel_multiplier=1)
         digit_no = small.tile([P, ANGLE_BITS], I32, name="digit_no")
@@ -62,6 +67,7 @@ def tile_attention_pa_kernel(
 
         HEAD_BLOCKS = 2
         HEAD_COLS = HEAD_BLOCKS * N_TILE
+        FIRST_PASSES = 3
 
         def load_head_codes(g):
             xc = keep.tile([P, 2 * 512], U8, name="x_codes%d" % g, align_bytes=64)
@@ -72,6 +78,11 @@ def tile_attention_pa_kernel(
             for n in range(HEAD_BLOCKS):
                 w_codes[(0, n, g)] = wc[:, 2 * N_TILE * n : 2 * N_TILE * (n + 1)]
 
+        def load_first_codes(n):
+            wc = keep.tile([P, 2 * N_TILE], U8, name="first_codes%d" % n, align_bytes=64)
+            load_codes(wc[:], wq_words[0][:, 2 * N_TILE * n : 2 * N_TILE * (n + 1)])
+            w_codes[(0, n, 0)] = wc
+
         def load_head_scales(g0, g1):
             xp = load_scales("x_planes%d" % g0, x_scales, g0, g1, 0, 512)
             wp = load_scales("head_planes%d" % g0, wq_scales, g0, g1, 0, HEAD_COLS)
@@ -80,11 +91,16 @@ def tile_attention_pa_kernel(
                 for n in range(HEAD_BLOCKS):
                     w_planes[(0, n, g)] = wp[:, g - g0, N_TILE * n : N_TILE * (n + 1)]
 
-        load_head_codes(0)
-        load_head_scales(0, 2)
-        load_head_codes(1)
-        load_head_scales(2, PASSES)
-        for g in range(2, PASSES):
+        xc0 = keep.tile([P, 2 * 512], U8, name="x_codes0", align_bytes=64)
+        load_codes(xc0[:], x_words[0])
+        x_codes[0] = xc0
+        load_first_codes(0)
+        load_first_codes(1)
+        load_head_scales(0, FIRST_PASSES)
+        for g in range(1, FIRST_PASSES):
+            load_head_codes(g)
+        load_head_scales(FIRST_PASSES, PASSES)
+        for g in range(FIRST_PASSES, PASSES):
             load_head_codes(g)
 
         def load_chunk(w, n0, blocks):
@@ -184,6 +200,10 @@ def tile_attention_pa_kernel(
                 out=outs[w][m].rearrange("t h d -> t (h d)")[:, first : first + cols],
                 in_=rot[:],
             )
+
+        idle = new_bank(N_TILE)
+        for i in range(WARM_UP):
+            nc.tensor.matmul(out=idle[:], lhsT=zeros[:, 0:P], rhs=zeros[:], start=True, stop=True)
 
         head = [(n, m) for n in range(HEAD_BLOCKS) for m in range(TOKEN_TILES)]
         banks = {}

@@ -178,12 +178,20 @@ def tile_attention_pa_kernel(
                 stop=(g == PASSES - 1),
             )
 
+        waiting = []
+
+        def store_waiting():
+            for dram_ap, tile_ap in waiting:
+                nc.scalar.dma_start(out=dram_ap, in_=tile_ap)
+            waiting.clear()
+
         def rotate_and_store(acc, w, n, m, c0, cols):
             half = cols // 2
             tag = turn("cross", 3)
             cross = turned.tile([P, 2, half], F32, name=tag, tag=tag)
             nc.scalar.activation(out=cross[:, 0, :], in_=acc[:, 1:cols:2], func=ACT.Copy, scale=neg_sin_p[:, 0:1])
             nc.scalar.activation(out=cross[:, 1, :], in_=acc[:, 0:cols:2], func=ACT.Copy, scale=sin_p[:, 0:1])
+            store_waiting()
             tag = turn("rot", 8)
             rot = result.tile([P, cols], F32, name=tag, tag=tag)
             nc.vector.scalar_tensor_tensor(
@@ -194,12 +202,12 @@ def tile_attention_pa_kernel(
                 op0=ALU.mult,
                 op1=ALU.add,
             )
-            queue = nc.sync if (w, n) == (1, BLOCKS - 1) else nc.gpsimd
             first = N_TILE * n + c0
-            queue.dma_start(
-                out=outs[w][m].rearrange("t h d -> t (h d)")[:, first : first + cols],
-                in_=rot[:],
-            )
+            dram_ap = outs[w][m].rearrange("t h d -> t (h d)")[:, first : first + cols]
+            if (w, n) == (1, BLOCKS - 1):
+                nc.sync.dma_start(out=dram_ap, in_=rot[:])
+            else:
+                waiting.append((dram_ap, rot[:]))
 
         idle = new_bank(N_TILE)
         for i in range(WARM_UP):

@@ -217,8 +217,11 @@ def tile_attention_pa_kernel(
         banks = {}
         for nm in head:
             banks[nm] = new_bank(N_TILE)
-        for g in range(PASSES):
+        for g in range(PASSES - 2):
             for n, m in head:
+                multiply(banks[(n, m)], 0, n, m, g, 0, N_TILE)
+        for n, m in head:
+            for g in range(PASSES - 2, PASSES):
                 multiply(banks[(n, m)], 0, n, m, g, 0, N_TILE)
         for n, m in head:
             rotate_and_store(banks[(n, m)], 0, n, m, 0, N_TILE)
@@ -229,8 +232,8 @@ def tile_attention_pa_kernel(
         for w, n in rest:
             for m in range(TOKEN_TILES):
                 last = (w, n, m) == (1, BLOCKS - 1, TOKEN_TILES - 1)
-                cols = N_TILE // 2 if last else N_TILE
-                for c0 in range(0, N_TILE, cols):
+                pieces = ((0, 256), (256, 128), (384, 128)) if last else ((0, N_TILE),)
+                for c0, cols in pieces:
                     acc = new_bank(cols)
                     for g in range(PASSES):
                         multiply(acc, w, n, m, g, c0, cols)

@@ -18,6 +18,7 @@ CHANNELS = 4096
 N_TILE = 512
 BLOCKS = CHANNELS // N_TILE
 ANGLE_BITS = 8
+W_PLANE_SHIFT = 64
 WARM_UP = 10
 
 FLOPS = 2 * 512 * 4096 * 2 * CHANNELS
@@ -42,9 +43,11 @@ def tile_attention_pa_kernel(
         def load_codes(tile_ap, dram_ap):
             nc.sync.dma_start(out=tile_ap.bitcast(I32), in_=dram_ap.bitcast(I32))
 
-        def load_scales(name, dram, g0, g1, c0, c1):
-            plane = keep.tile([P, g1 - g0, c1 - c0], U8, name=name, align_bytes=64)
-            nc.vector.memset(plane[:].bitcast(I32), 0)
+        def load_scales(name, dram, g0, g1, c0, c1, shift):
+            size = (g1 - g0) * (c1 - c0)
+            room = keep.tile([P, size + 256], U8, name=name, align_bytes=256)
+            nc.vector.memset(room[:].bitcast(I32), 0)
+            plane = room[:, shift : shift + size].rearrange("p (g c) -> p g c", g=g1 - g0)
             for q in (0, 2, 1, 3):
                 nc.sync.dma_start(
                     out=plane[32 * q : 32 * q + 4, :, :].bitcast(I32),
@@ -70,28 +73,28 @@ def tile_attention_pa_kernel(
         FIRST_PASSES = 3
 
         def load_head_codes(g):
-            xc = keep.tile([P, 2 * 512], U8, name="x_codes%d" % g, align_bytes=64)
+            xc = keep.tile([P, 2 * 512], U8, name="x_codes%d" % g, align_bytes=256)
             load_codes(xc[:], x_words[g])
             x_codes[g] = xc
-            wc = keep.tile([P, 2 * HEAD_COLS], U8, name="head_codes%d" % g, align_bytes=64)
+            wc = keep.tile([P, 2 * HEAD_COLS], U8, name="head_codes%d" % g, align_bytes=256)
             load_codes(wc[:], wq_words[g][:, 0 : 2 * HEAD_COLS])
             for n in range(HEAD_BLOCKS):
                 w_codes[(0, n, g)] = wc[:, 2 * N_TILE * n : 2 * N_TILE * (n + 1)]
 
         def load_first_codes(n):
-            wc = keep.tile([P, 2 * N_TILE], U8, name="first_codes%d" % n, align_bytes=64)
+            wc = keep.tile([P, 2 * N_TILE], U8, name="first_codes%d" % n, align_bytes=256)
             load_codes(wc[:], wq_words[0][:, 2 * N_TILE * n : 2 * N_TILE * (n + 1)])
             w_codes[(0, n, 0)] = wc
 
         def load_head_scales(g0, g1):
-            xp = load_scales("x_planes%d" % g0, x_scales, g0, g1, 0, 512)
-            wp = load_scales("head_planes%d" % g0, wq_scales, g0, g1, 0, HEAD_COLS)
+            xp = load_scales("x_planes%d" % g0, x_scales, g0, g1, 0, 512, 0)
+            wp = load_scales("head_planes%d" % g0, wq_scales, g0, g1, 0, HEAD_COLS, W_PLANE_SHIFT)
             for g in range(g0, g1):
                 x_planes[g] = xp[:, g - g0, :]
                 for n in range(HEAD_BLOCKS):
                     w_planes[(0, n, g)] = wp[:, g - g0, N_TILE * n : N_TILE * (n + 1)]
 
-        xc0 = keep.tile([P, 2 * 512], U8, name="x_codes0", align_bytes=64)
+        xc0 = keep.tile([P, 2 * 512], U8, name="x_codes0", align_bytes=256)
         load_codes(xc0[:], x_words[0])
         x_codes[0] = xc0
         load_first_codes(0)
@@ -106,8 +109,8 @@ def tile_attention_pa_kernel(
         def load_chunk(w, n0, blocks):
             c0 = N_TILE * n0
             c1 = N_TILE * (n0 + blocks)
-            wp = load_scales("planes%d_%d" % (w, n0), w_scales[w], 0, PASSES, c0, c1)
-            wc = keep.tile([P, PASSES, 2 * (c1 - c0)], U8, name="codes%d_%d" % (w, n0), align_bytes=64)
+            wp = load_scales("planes%d_%d" % (w, n0), w_scales[w], 0, PASSES, c0, c1, W_PLANE_SHIFT)
+            wc = keep.tile([P, PASSES, 2 * (c1 - c0)], U8, name="codes%d_%d" % (w, n0), align_bytes=256)
             load_codes(wc[:], w_words[w][:, :, 2 * c0 : 2 * c1].rearrange("g p c -> p g c"))
             for n in range(blocks):
                 for g in range(PASSES):

@@ -19,6 +19,7 @@ N_TILE = 512
 BLOCKS = CHANNELS // N_TILE
 ANGLE_BITS = 8
 W_PLANE_SHIFT = 64
+X_PLANE_SHIFT = 64
 WARM_UP = 10
 
 FLOPS = 2 * 512 * 4096 * 2 * CHANNELS
@@ -87,7 +88,7 @@ def tile_attention_pa_kernel(
             w_codes[(0, n, 0)] = wc
 
         def load_head_scales(g0, g1):
-            xp = load_scales("x_planes%d" % g0, x_scales, g0, g1, 0, 512, 0)
+            xp = load_scales("x_planes%d" % g0, x_scales, g0, g1, 0, 512, X_PLANE_SHIFT)
             wp = load_scales("head_planes%d" % g0, wq_scales, g0, g1, 0, HEAD_COLS, W_PLANE_SHIFT)
             for g in range(g0, g1):
                 x_planes[g] = xp[:, g - g0, :]

@@ -18,8 +18,8 @@ CHANNELS = 4096
 N_TILE = 512
 BLOCKS = CHANNELS // N_TILE
 ANGLE_BITS = 8
-W_PLANE_SHIFT = 64
-X_PLANE_SHIFT = 64
+W_PLANE_SHIFT = 0
+X_PLANE_SHIFT = 0
 WARM_UP = 10
 
 FLOPS = 2 * 512 * 4096 * 2 * CHANNELS

@@ -62,12 +62,7 @@ def tile_attention_pa_kernel(
         w_planes = {}
 
         zeros = small.tile([P, N_TILE], BF16, name="zeros")
-        nc.gpsimd.memset(zeros[:], 0.0)
-
-        position = small.tile([P, ANGLE_BITS], I32, name="position")
-        nc.gpsimd.iota(position[:], pattern=[[0, ANGLE_BITS]], base=0, channel_multiplier=1)
-        digit_no = small.tile([P, ANGLE_BITS], I32, name="digit_no")
-        nc.gpsimd.iota(digit_no[:], pattern=[[1, ANGLE_BITS]], base=0, channel_multiplier=0)
+        nc.vector.memset(zeros[:], 0.0)
 
         HEAD_BLOCKS = 2
         HEAD_COLS = HEAD_BLOCKS * N_TILE
@@ -119,6 +114,13 @@ def tile_attention_pa_kernel(
                     w_planes[(w, n0 + n, g)] = wp[:, g, N_TILE * n : N_TILE * (n + 1)]
 
         load_chunk(0, 2, 2)
+
+        position = small.tile([P, ANGLE_BITS], I32, name="position")
+        nc.vector.memset(position[:], 0)
+        nc.gpsimd.iota(position[:], pattern=[[0, ANGLE_BITS]], base=0, channel_multiplier=1)
+        digit_no = small.tile([P, ANGLE_BITS], I32, name="digit_no")
+        nc.vector.memset(digit_no[:], 0)
+        nc.gpsimd.iota(digit_no[:], pattern=[[1, ANGLE_BITS]], base=0, channel_multiplier=0)
 
         shifted = small.tile([P, ANGLE_BITS], I32, name="shifted")
         nc.vector.tensor_tensor(out=shifted[:], in0=position[:], in1=digit_no[:], op=ALU.logical_shift_right)

@@ -44,16 +44,22 @@ def tile_attention_pa_kernel(
         def load_codes(tile_ap, dram_ap):
             nc.sync.dma_start(out=tile_ap.bitcast(I32), in_=dram_ap.bitcast(I32))
 
-        def load_scales(name, dram, g0, g1, c0, c1, shift):
+        def new_planes(name, g0, g1, c0, c1, shift):
             size = (g1 - g0) * (c1 - c0)
             room = keep.tile([P, size + 256], U8, name=name, align_bytes=256)
             nc.vector.memset(room[:].bitcast(I32), 0)
-            plane = room[:, shift : shift + size].rearrange("p (g c) -> p g c", g=g1 - g0)
-            for q in (0, 2, 1, 3):
+            return room[:, shift : shift + size].rearrange("p (g c) -> p g c", g=g1 - g0)
+
+        def fill_planes(plane, dram, g0, g1, c0, c1, quadrants):
+            for q in quadrants:
                 nc.sync.dma_start(
                     out=plane[32 * q : 32 * q + 4, :, :].bitcast(I32),
                     in_=dram[g0:g1, 4 * q : 4 * q + 4, c0:c1].rearrange("g r n -> r g n").bitcast(I32),
                 )
+
+        def load_scales(name, dram, g0, g1, c0, c1, shift):
+            plane = new_planes(name, g0, g1, c0, c1, shift)
+            fill_planes(plane, dram, g0, g1, c0, c1, (0, 2, 1, 3))
             return plane
 
         x_codes = {}
@@ -61,8 +67,6 @@ def tile_attention_pa_kernel(
         w_codes = {}
         w_planes = {}
 
-        zeros = small.tile([P, N_TILE], BF16, name="zeros")
-        nc.vector.memset(zeros[:], 0.0)
 
         HEAD_BLOCKS = 2
         HEAD_COLS = HEAD_BLOCKS * N_TILE
@@ -94,8 +98,18 @@ def tile_attention_pa_kernel(
         load_codes(xc0[:], x_words[0])
         x_codes[0] = xc0
         load_first_codes(0)
+        xp0 = new_planes("x_planes0", 0, FIRST_PASSES, 0, 512, X_PLANE_SHIFT)
+        zeros = small.tile([P, N_TILE], BF16, name="zeros")
+        nc.vector.memset(zeros[:], 0.0)
+        wp0 = new_planes("head_planes0", 0, FIRST_PASSES, 0, HEAD_COLS, W_PLANE_SHIFT)
+        fill_planes(xp0, x_scales, 0, FIRST_PASSES, 0, 512, (0, 2))
+        fill_planes(wp0, wq_scales, 0, FIRST_PASSES, 0, HEAD_COLS, (0, 2, 1, 3))
+        fill_planes(xp0, x_scales, 0, FIRST_PASSES, 0, 512, (1, 3))
         load_first_codes(1)
-        load_head_scales(0, FIRST_PASSES)
+        for g in range(FIRST_PASSES):
+            x_planes[g] = xp0[:, g, :]
+            for n in range(HEAD_BLOCKS):
+                w_planes[(0, n, g)] = wp0[:, g, N_TILE * n : N_TILE * (n + 1)]
         for g in range(1, FIRST_PASSES):
             load_head_codes(g)
         load_head_scales(FIRST_PASSES, PASSES)

@@ -20,7 +20,7 @@ BLOCKS = CHANNELS // N_TILE
 ANGLE_BITS = 8
 W_PLANE_SHIFT = 0
 X_PLANE_SHIFT = 0
-WARM_UP = 10
+WARM_UP = 7
 
 FLOPS = 2 * 512 * 4096 * 2 * CHANNELS
 

import math
from contextlib import ExitStack

import concourse.mybir as mybir

F32 = mybir.dt.float32
BF16 = mybir.dt.bfloat16
I32 = mybir.dt.int32
U8 = mybir.dt.uint8
FP4X4 = mybir.dt.float4_e2m1fn_x4
ALU = mybir.AluOpType
ACT = mybir.ActivationFunctionType

P = 128
PASSES = 8
TOKEN_TILES = 4
CHANNELS = 4096
N_TILE = 512
BLOCKS = CHANNELS // N_TILE
ANGLE_BITS = 8
W_PLANE_SHIFT = 0
X_PLANE_SHIFT = 0
WARM_UP = 7

FLOPS = 2 * 512 * 4096 * 2 * CHANNELS


def tile_attention_pa_kernel(
    tc, x_words, x_scales, wq_words, wq_scales, wk_words, wk_scales, out_0, out_1
):
    nc = tc.nc
    w_words = (wq_words, wk_words)
    w_scales = (wq_scales, wk_scales)
    outs = (out_0, out_1)

    with ExitStack() as ctx:
        keep = ctx.enter_context(tc.tile_pool(name="keep", bufs=1))
        small = ctx.enter_context(tc.tile_pool(name="small", bufs=1))
        turned = ctx.enter_context(tc.tile_pool(name="turned", bufs=1))
        result = ctx.enter_context(tc.tile_pool(name="result", bufs=1))
        psum = ctx.enter_context(tc.psum_pool(name="psum", bufs=1))
        ctx.enter_context(tc.manual_schedule())

        def load_codes(tile_ap, dram_ap):
            nc.sync.dma_start(out=tile_ap.bitcast(I32), in_=dram_ap.bitcast(I32))

        def new_planes(name, g0, g1, c0, c1, shift):
            size = (g1 - g0) * (c1 - c0)
            room = keep.tile([P, size + 256], U8, name=name, align_bytes=256)
            nc.vector.memset(room[:].bitcast(I32), 0)
            return room[:, shift : shift + size].rearrange("p (g c) -> p g c", g=g1 - g0)

        def fill_planes(plane, dram, g0, g1, c0, c1, quadrants):
            for q in quadrants:
                nc.sync.dma_start(
                    out=plane[32 * q : 32 * q + 4, :, :].bitcast(I32),
                    in_=dram[g0:g1, 4 * q : 4 * q + 4, c0:c1].rearrange("g r n -> r g n").bitcast(I32),
                )

        def load_scales(name, dram, g0, g1, c0, c1, shift):
            plane = new_planes(name, g0, g1, c0, c1, shift)
            fill_planes(plane, dram, g0, g1, c0, c1, (0, 2, 1, 3))
            return plane

        x_codes = {}
        x_planes = {}
        w_codes = {}
        w_planes = {}


        HEAD_BLOCKS = 2
        HEAD_COLS = HEAD_BLOCKS * N_TILE
        FIRST_PASSES = 3

        def load_head_codes(g):
            xc = keep.tile([P, 2 * 512], U8, name="x_codes%d" % g, align_bytes=256)
            load_codes(xc[:], x_words[g])
            x_codes[g] = xc
            wc = keep.tile([P, 2 * HEAD_COLS], U8, name="head_codes%d" % g, align_bytes=256)
            load_codes(wc[:], wq_words[g][:, 0 : 2 * HEAD_COLS])
            for n in range(HEAD_BLOCKS):
                w_codes[(0, n, g)] = wc[:, 2 * N_TILE * n : 2 * N_TILE * (n + 1)]

        def load_first_codes(n):
            wc = keep.tile([P, 2 * N_TILE], U8, name="first_codes%d" % n, align_bytes=256)
            load_codes(wc[:], wq_words[0][:, 2 * N_TILE * n : 2 * N_TILE * (n + 1)])
            w_codes[(0, n, 0)] = wc

        def load_head_scales(g0, g1):
            xp = load_scales("x_planes%d" % g0, x_scales, g0, g1, 0, 512, X_PLANE_SHIFT)
            wp = load_scales("head_planes%d" % g0, wq_scales, g0, g1, 0, HEAD_COLS, W_PLANE_SHIFT)
            for g in range(g0, g1):
                x_planes[g] = xp[:, g - g0, :]
                for n in range(HEAD_BLOCKS):
                    w_planes[(0, n, g)] = wp[:, g - g0, N_TILE * n : N_TILE * (n + 1)]

        xc0 = keep.tile([P, 2 * 512], U8, name="x_codes0", align_bytes=256)
        load_codes(xc0[:], x_words[0])
        x_codes[0] = xc0
        load_first_codes(0)
        xp0 = new_planes("x_planes0", 0, FIRST_PASSES, 0, 512, X_PLANE_SHIFT)
        zeros = small.tile([P, N_TILE], BF16, name="zeros")
        nc.vector.memset(zeros[:], 0.0)
        wp0 = new_planes("head_planes0", 0, FIRST_PASSES, 0, HEAD_COLS, W_PLANE_SHIFT)
        fill_planes(xp0, x_scales, 0, FIRST_PASSES, 0, 512, (0, 2))
        fill_planes(wp0, wq_scales, 0, FIRST_PASSES, 0, HEAD_COLS, (0, 2, 1, 3))
        fill_planes(xp0, x_scales, 0, FIRST_PASSES, 0, 512, (1, 3))
        load_first_codes(1)
        for g in range(FIRST_PASSES):
            x_planes[g] = xp0[:, g, :]
            for n in range(HEAD_BLOCKS):
                w_planes[(0, n, g)] = wp0[:, g, N_TILE * n : N_TILE * (n + 1)]
        for g in range(1, FIRST_PASSES):
            load_head_codes(g)
        load_head_scales(FIRST_PASSES, PASSES)
        for g in range(FIRST_PASSES, PASSES):
            load_head_codes(g)

        def load_chunk(w, n0, blocks):
            c0 = N_TILE * n0
            c1 = N_TILE * (n0 + blocks)
            wp = load_scales("planes%d_%d" % (w, n0), w_scales[w], 0, PASSES, c0, c1, W_PLANE_SHIFT)
            wc = keep.tile([P, PASSES, 2 * (c1 - c0)], U8, name="codes%d_%d" % (w, n0), align_bytes=256)
            load_codes(wc[:], w_words[w][:, :, 2 * c0 : 2 * c1].rearrange("g p c -> p g c"))
            for n in range(blocks):
                for g in range(PASSES):
                    w_codes[(w, n0 + n, g)] = wc[:, g, 2 * N_TILE * n : 2 * N_TILE * (n + 1)]
                    w_planes[(w, n0 + n, g)] = wp[:, g, N_TILE * n : N_TILE * (n + 1)]

        load_chunk(0, 2, 2)

        position = small.tile([P, ANGLE_BITS], I32, name="position")
        nc.vector.memset(position[:], 0)
        nc.gpsimd.iota(position[:], pattern=[[0, ANGLE_BITS]], base=0, channel_multiplier=1)
        digit_no = small.tile([P, ANGLE_BITS], I32, name="digit_no")
        nc.vector.memset(digit_no[:], 0)
        nc.gpsimd.iota(digit_no[:], pattern=[[1, ANGLE_BITS]], base=0, channel_multiplier=0)

        shifted = small.tile([P, ANGLE_BITS], I32, name="shifted")
        nc.vector.tensor_tensor(out=shifted[:], in0=position[:], in1=digit_no[:], op=ALU.logical_shift_right)
        digit_i = small.tile([P, ANGLE_BITS], I32, name="digit_i")
        nc.vector.tensor_scalar(out=digit_i[:], in0=shifted[:], scalar1=1, scalar2=None, op0=ALU.bitwise_and)
        digit = small.tile([P, ANGLE_BITS], F32, name="digit")
        nc.vector.tensor_copy(out=digit[:], in_=digit_i[:])
        re = small.tile([P, ANGLE_BITS], F32, name="re8")
        im = small.tile([P, ANGLE_BITS], F32, name="im8")
        for b in range(ANGLE_BITS):
            angle = 2.0**b
            nc.vector.tensor_scalar(
                out=re[:, b : b + 1], in0=digit[:, b : b + 1],
                scalar1=math.cos(angle) - 1.0, scalar2=1.0, op0=ALU.mult, op1=ALU.add,
            )
            nc.vector.tensor_scalar(
                out=im[:, b : b + 1], in0=digit[:, b : b + 1],
                scalar1=math.sin(angle), scalar2=None, op0=ALU.mult,
            )
        width = ANGLE_BITS // 2
        while width >= 1:
            a_re, a_im = re[:, 0:width], im[:, 0:width]
            b_re, b_im = re[:, width : 2 * width], im[:, width : 2 * width]
            rr = small.tile([P, width], F32, name="rr%d" % width)
            ii = small.tile([P, width], F32, name="ii%d" % width)
            ri = small.tile([P, width], F32, name="ri%d" % width)
            ir = small.tile([P, width], F32, name="ir%d" % width)
            nc.vector.tensor_tensor(out=rr[:], in0=a_re, in1=b_re, op=ALU.mult)
            nc.vector.tensor_tensor(out=ii[:], in0=a_im, in1=b_im, op=ALU.mult)
            nc.vector.tensor_tensor(out=ri[:], in0=a_re, in1=b_im, op=ALU.mult)
            nc.vector.tensor_tensor(out=ir[:], in0=a_im, in1=b_re, op=ALU.mult)
            re = small.tile([P, width], F32, name="re%d" % width)
            im = small.tile([P, width], F32, name="im%d" % width)
            nc.vector.tensor_tensor(out=re[:], in0=rr[:], in1=ii[:], op=ALU.subtract)
            nc.vector.tensor_tensor(out=im[:], in0=ri[:], in1=ir[:], op=ALU.add)
            width //= 2
        cos_p = re
        sin_p = im
        neg_sin_p = small.tile([P, 1], F32, name="neg_sin_p")
        nc.scalar.activation(out=neg_sin_p[:], in_=sin_p[:], func=ACT.Copy, scale=-1.0)

        counts = {"bank": 0, "cross": 0, "rot": 0}

        def turn(kind, slots):
            counts[kind] += 1
            return "%s%d" % (kind, (counts[kind] - 1) % slots)

        def new_bank(cols):
            tag = turn("bank", 8)
            acc = psum.tile([P, cols], F32, name=tag, tag=tag)
            return acc

        def multiply(acc, w, n, m, g, c0, cols):
            nc.tensor.matmul_mx(
                out=acc[:],
                lhsT=x_codes[g][:, 2 * P * m : 2 * P * (m + 1)].bitcast(FP4X4),
                lhsT_scale=x_planes[g][:, P * m : P * (m + 1)],
                rhs=w_codes[(w, n, g)][:, 2 * c0 : 2 * (c0 + cols)].bitcast(FP4X4),
                rhs_scale=w_planes[(w, n, g)][:, c0 : c0 + cols],
                start=(g == 0),
                stop=(g == PASSES - 1),
            )

        waiting = []

        def store_waiting():
            for dram_ap, tile_ap in waiting:
                nc.scalar.dma_start(out=dram_ap, in_=tile_ap)
            waiting.clear()

        def rotate_and_store(acc, w, n, m, c0, cols):
            half = cols // 2
            tag = turn("cross", 3)
            cross = turned.tile([P, 2, half], F32, name=tag, tag=tag)
            nc.scalar.activation(out=cross[:, 0, :], in_=acc[:, 1:cols:2], func=ACT.Copy, scale=neg_sin_p[:, 0:1])
            nc.scalar.activation(out=cross[:, 1, :], in_=acc[:, 0:cols:2], func=ACT.Copy, scale=sin_p[:, 0:1])
            store_waiting()
            tag = turn("rot", 8)
            rot = result.tile([P, cols], F32, name=tag, tag=tag)
            nc.vector.scalar_tensor_tensor(
                out=rot[:].rearrange("p (i j) -> p i j", j=2),
                in0=acc[:].rearrange("p (i j) -> p i j", j=2),
                scalar=cos_p[:, 0:1],
                in1=cross[:].rearrange("p j i -> p i j"),
                op0=ALU.mult,
                op1=ALU.add,
            )
            first = N_TILE * n + c0
            dram_ap = outs[w][m].rearrange("t h d -> t (h d)")[:, first : first + cols]
            if (w, n) == (1, BLOCKS - 1):
                nc.sync.dma_start(out=dram_ap, in_=rot[:])
            else:
                waiting.append((dram_ap, rot[:]))

        idle = new_bank(N_TILE)
        for i in range(WARM_UP):
            nc.tensor.matmul(out=idle[:], lhsT=zeros[:, 0:P], rhs=zeros[:], start=True, stop=True)

        head = [(n, m) for n in range(HEAD_BLOCKS) for m in range(TOKEN_TILES)]
        banks = {}
        for nm in head:
            banks[nm] = new_bank(N_TILE)
        for g in range(PASSES - 2):
            for n, m in head:
                multiply(banks[(n, m)], 0, n, m, g, 0, N_TILE)
        for n, m in head:
            for g in range(PASSES - 2, PASSES):
                multiply(banks[(n, m)], 0, n, m, g, 0, N_TILE)
        for n, m in head:
            rotate_and_store(banks[(n, m)], 0, n, m, 0, N_TILE)
            if (n, m) == (0, 0):
                load_chunk(0, 4, 2)

        rest = [(0, n) for n in range(HEAD_BLOCKS, BLOCKS)] + [(1, n) for n in range(BLOCKS)]
        for w, n in rest:
            for m in range(TOKEN_TILES):
                last = (w, n, m) == (1, BLOCKS - 1, TOKEN_TILES - 1)
                pieces = ((0, 256), (256, 128), (384, 128)) if last else ((0, N_TILE),)
                for c0, cols in pieces:
                    acc = new_bank(cols)
                    for g in range(PASSES):
                        multiply(acc, w, n, m, g, c0, cols)
                    rotate_and_store(acc, w, n, m, c0, cols)
                sweep = BLOCKS * w + n
                if m == 0 and sweep % 2 == 1 and sweep + 3 < 2 * BLOCKS:
                    load_chunk((sweep + 3) // BLOCKS, (sweep + 3) % BLOCKS, 2)
